import numpy as np
import ml_dtypes


def mxq(x, axis, fmt="e4m3"):
    dtype, down = {"e4m3": (ml_dtypes.float8_e4m3fn, 7), "e5m2": (ml_dtypes.float8_e5m2, 14)}[fmt]
    v = np.moveaxis(np.asarray(x, np.float32).astype(ml_dtypes.bfloat16).astype(np.float64), axis, -1)
    blocks = v.reshape(v.shape[:-1] + (-1, 32))
    amax = np.abs(blocks).max(-1, keepdims=True)
    byte = np.maximum(np.where(amax > 0, np.frexp(amax)[1] - 1 + 127, 0) - down, 1)
    scale = np.exp2(byte - 127.0)
    codes = (blocks / scale).astype(np.float32).astype(dtype).astype(np.float64)
    return np.moveaxis((codes * scale).reshape(v.shape), -1, axis)


WIDE = False


def mx_kscale(k):
    if not WIDE:
        return np.ones(k)
    levels = np.array([10, -10, 5, -5, 0])
    a = np.random.permutation(np.resize(levels, k // 512 * 4)).reshape(k // 512, 4)
    idx = np.arange(k)
    return np.exp2(a[idx // 512, idx % 128 // 32])


BF16 = ml_dtypes.bfloat16


def bf(x):
    return np.asarray(x, np.float32).astype(BF16)


def f64(x):
    return np.asarray(x).astype(np.float64)


B, N, E, H, NOPE, VDIM, ROPE, QR, KVR = 4, 256, 2048, 16, 128, 128, 128, 512, 512
QH = NOPE + ROPE
BASE = 10000.0


def rope(v):
    d = v.shape[-1]
    n = v.shape[-2]
    theta = BASE ** (-2.0 * np.arange(d // 2) / d)
    ang = np.arange(n)[:, None] * theta[None, :]
    cos, sin = np.cos(ang), np.sin(ang)
    v1, v2 = v[..., 0::2], v[..., 1::2]
    return np.stack([v1 * cos - v2 * sin, v1 * sin + v2 * cos], axis=-1).reshape(v.shape)


def setup_inputs():
    s, t = mx_kscale(E), mx_kscale(QR)
    return {"x": bf(np.random.standard_normal((B, N, E)) * s),
            "Wqa": bf(np.random.standard_normal((E, QR)) / np.sqrt(E) / s[:, None] * t),
            "Wqb": bf(np.random.standard_normal((QR, H * QH)) / np.sqrt(QR) / t[:, None])}


def reference(x, Wqa, Wqb):
    cq = mxq(f64(x), 2, "e4m3") @ mxq(f64(Wqa), 0, "e4m3")
    q = mxq(cq, 2, "e4m3") @ mxq(f64(Wqb), 0, "e4m3")
    q = q.reshape(B, N, H, QH).transpose(0, 2, 1, 3)
    return np.concatenate([q[..., :NOPE], rope(q[..., NOPE:])], axis=-1)

@@ -1,0 +1,306 @@
+import math
+from contextlib import ExitStack
+
+import concourse.masks as masks
+import concourse.mybir as mybir
+
+F32 = mybir.dt.float32
+BF16 = mybir.dt.bfloat16
+U32 = mybir.dt.uint32
+U8 = mybir.dt.uint8
+I32 = mybir.dt.int32
+FP8X4 = mybir.dt.float8_e4m3fn_x4
+ALU = mybir.AluOpType
+ACT = mybir.ActivationFunctionType
+
+P = 128
+B, N, E, H, QR = 4, 256, 2048, 16, 512
+NOPE, ROPE = 128, 128
+QH = NOPE + ROPE
+BASE = 10000.0
+S = 8
+G1 = E // 512
+HG = 4
+NG = H // HG
+FREQ = ROPE // 2
+
+FLOPS = 2 * B * N * E * QR + 2 * B * N * QR * H * QH
+
+
+def tile_multilatentattention_pa_kernel(tc, x, Wqa, Wqb, out):
+    nc = tc.nc
+    with ExitStack() as ctx:
+        keep = ctx.enter_context(tc.tile_pool(name="keep", bufs=1))
+        work = ctx.enter_context(tc.tile_pool(name="work", bufs=2))
+        psum = ctx.enter_context(tc.psum_pool(name="psum", bufs=8))
+
+        ident = keep.tile([P, P], F32, name="ident")
+        masks.make_identity(nc, ident[:])
+
+        two_p = keep.tile([P, S], I32, name="two_p")
+        nc.gpsimd.iota(two_p[:], pattern=[[0, S]], base=0, channel_multiplier=2)
+        s_idx = keep.tile([P, S], I32, name="s_idx")
+        nc.gpsimd.iota(s_idx[:], pattern=[[1, S]], base=0, channel_multiplier=0)
+        nc.vector.tensor_single_scalar(out=two_p[:], in_=two_p[:], scalar=248, op=ALU.bitwise_and)
+        pos_a = keep.tile([P, S], F32, name="pos_a")
+        nc.vector.tensor_copy(out=pos_a[:], in_=two_p[:])
+        pos_b = keep.tile([P, S], F32, name="pos_b")
+        nc.vector.tensor_copy(out=pos_b[:], in_=s_idx[:])
+        nc.vector.tensor_tensor(out=pos_a[:], in0=pos_a[:], in1=pos_b[:], op=ALU.add)
+        nc.vector.tensor_scalar_mul(out=pos_a[:], in0=pos_a[:], scalar1=1.0 / (2.0 * math.pi))
+
+        theta = keep.tile([P, FREQ], F32, name="theta")
+        nc.vector.memset(theta[:, 0:1], 1.0)
+        for j in range(6):
+            w = 1 << j
+            nc.vector.tensor_scalar_mul(
+                out=theta[:, w : 2 * w], in0=theta[:, 0:w], scalar1=BASE ** (-2.0 * w / ROPE)
+            )
+
+        turns = keep.tile([P, S, FREQ], F32, name="turns")
+        nc.gpsimd.tensor_tensor(
+            out=turns[:],
+            in0=theta[:].unsqueeze(1).to_broadcast([P, S, FREQ]),
+            in1=pos_a[:].unsqueeze(2).to_broadcast([P, S, FREQ]),
+            op=ALU.mult,
+        )
+        whole_i = keep.tile([P, S, FREQ], I32, name="whole_i")
+        nc.vector.tensor_copy(out=whole_i[:], in_=turns[:])
+        whole_f = keep.tile([P, S, FREQ], F32, name="whole_f")
+        nc.vector.tensor_copy(out=whole_f[:], in_=whole_i[:])
+        nc.gpsimd.tensor_tensor(out=turns[:], in0=turns[:], in1=whole_f[:], op=ALU.subtract)
+        turns_c = keep.tile([P, S, FREQ], F32, name="turns_c")
+        nc.gpsimd.tensor_scalar(
+            out=turns_c[:], in0=turns[:], scalar1=1.0, scalar2=0.25, op0=ALU.mult, op1=ALU.add
+        )
+        planes = keep.tile([P, 3, S * FREQ], F32, name="planes")
+        nc.vector.scalar_tensor_tensor(
+            out=planes[:, 2, :],
+            in0=turns[:].rearrange("p s m -> p (s m)"),
+            scalar=0.5,
+            in1=turns[:].rearrange("p s m -> p (s m)"),
+            op0=ALU.is_gt,
+            op1=ALU.subtract,
+        )
+        nc.vector.scalar_tensor_tensor(
+            out=planes[:, 1, :],
+            in0=turns_c[:].rearrange("p s m -> p (s m)"),
+            scalar=0.5,
+            in1=turns_c[:].rearrange("p s m -> p (s m)"),
+            op0=ALU.is_gt,
+            op1=ALU.subtract,
+        )
+        nc.gpsimd.tensor_scalar(
+            out=planes[:, 0, :], in0=planes[:, 2, :], scalar1=-1.0, scalar2=0.0, op0=ALU.mult, op1=ALU.add
+        )
+        cos_sin = keep.tile([P, S, FREQ, 2], F32, name="cos_sin")
+        nsin_cos = keep.tile([P, S, FREQ, 2], F32, name="nsin_cos")
+        nc.scalar.activation(
+            out=cos_sin[:].rearrange("p s m e -> p (s m) e"),
+            in_=planes[:, 1:3, :].rearrange("p e x -> p x e"),
+            func=ACT.Sin,
+            scale=-2.0 * math.pi,
+        )
+        nc.scalar.activation(
+            out=nsin_cos[:].rearrange("p s m e -> p (s m) e"),
+            in_=planes[:, 0:2, :].rearrange("p e x -> p x e"),
+            func=ACT.Sin,
+            scale=-2.0 * math.pi,
+        )
+
+        wa_codes = keep.tile([P, G1, QR], U32, name="wa_codes", align_bytes=64)
+        wa_scale = keep.tile([P, G1, QR], U8, name="wa_scale", align_bytes=64)
+        x_codes = keep.tile([P, S, G1 * P], U32, name="x_codes", align_bytes=64)
+        x_scale = keep.tile([P, S, G1 * P], U8, name="x_scale", align_bytes=64)
+        cq_codes = keep.tile([P, S, P], U32, name="cq_codes", align_bytes=64)
+        cq_scale = keep.tile([P, S, P], U8, name="cq_scale", align_bytes=64)
+        wb_codes = keep.tile([P, NG, 2, 512], U32, name="wb_codes", align_bytes=64)
+        wb_scale = keep.tile([P, NG, 2, 512], U8, name="wb_scale", align_bytes=64)
+
+        wa_raw = work.tile([P, G1, 2, 1024], BF16, name="wa_raw", tag="big16", bufs=3)
+        for g in range(G1):
+            nc.sync.dma_start(
+                out=wa_raw[:, g],
+                in_=Wqa[512 * g : 512 * (g + 1), :].rearrange("(u p e) c -> p u (e c)", u=2, e=2),
+            )
+        x_view = x.rearrange("b (q s) k -> b q s k", s=S)
+        x_raw = []
+        wb_raw = []
+
+        def load_x(sq):
+            xs = work.tile([P, 2, E], BF16, name="x_raw%d" % sq, tag="raw8", bufs=6)
+            for b in range(B):
+                nc.sync.dma_start(out=xs[b::4, :, :], in_=x_view[b, :, 2 * sq : 2 * sq + 2, :])
+            x_raw.append(xs)
+
+        def load_wb(g):
+            wb = work.tile([P, 4, 1024], BF16, name="wb_raw%d" % g, tag="raw8", bufs=6)
+            nc.sync.dma_start(
+                out=wb[:], in_=Wqb[:, 1024 * g : 1024 * (g + 1)].rearrange("(t p) c -> p t c", t=4)
+            )
+            wb_raw.append(wb)
+
+        load_x(0)
+        load_x(1)
+        load_wb(0)
+        load_x(2)
+        load_x(3)
+        load_wb(1)
+        load_wb(2)
+        load_wb(3)
+
+        wa_grouped = []
+
+        def wa_regroup(g):
+            wag = work.tile([P, QR, 4], BF16, name="wag%d" % g, tag="wag", bufs=2, align_bytes=64)
+            src = wa_raw[:, g].rearrange("p u (e c) -> p (u e) c", e=2)
+            nc.vector.tensor_copy(
+                out=wag[:].rearrange("p (c i) t -> p c t i", i=4),
+                in_=src.rearrange("p t (c i) -> p c t i", i=4),
+            )
+            wa_grouped.append(wag)
+
+        def wa_quant(g):
+            nc.vector.quantize_mx(
+                out=wa_codes[:, g, :].bitcast(FP8X4),
+                scales=wa_scale[:, g, :],
+                in_=wa_grouped[g][:].rearrange("p c t -> p (c t)"),
+            )
+
+        wa_regroup(0)
+        for g in range(1, G1):
+            wa_regroup(g)
+            wa_quant(g - 1)
+        wa_quant(G1 - 1)
+
+        x_grouped = {}
+        cq_grouped = {}
+
+        def transpose_x(s):
+            words = x_raw[s // 2][:].bitcast(F32)
+            xg = work.tile([P, G1, P, 4], BF16, name="xg%d" % s, tag="xg", bufs=3, align_bytes=64)
+            xg_words = xg[:].bitcast(F32)
+            for half in range(2):
+                xt = psum.tile([P, 2, 2, P], F32, name="xt", tag="ps")
+                for gg in range(2):
+                    for u in range(2):
+                        col = 256 * (2 * half + gg) + 128 * u
+                        nc.tensor.transpose(
+                            out=xt[:, gg, u, :], in_=words[:, s % 2, col : col + P], identity=ident[:]
+                        )
+                nc.scalar.copy(
+                    out=xg_words[:, 2 * half : 2 * half + 2, :, :],
+                    in_=xt[:].rearrange("p g u t -> p g t u"),
+                )
+            x_grouped[s] = xg
+
+        def quant_x(s):
+            nc.vector.quantize_mx(
+                out=x_codes[:, s, :].bitcast(FP8X4),
+                scales=x_scale[:, s, :],
+                in_=x_grouped[s][:].rearrange("p g t j -> p (g t j)"),
+            )
+
+        def first_matmul(s):
+            cqp = psum.tile([P, 4, P], F32, name="cqp", tag="ps")
+            for c in range(4):
+                for g in range(G1):
+                    nc.tensor.matmul_mx(
+                        out=cqp[:, c, :],
+                        lhsT=wa_codes[:, g, P * c : P * (c + 1)].bitcast(FP8X4),
+                        lhsT_scale=wa_scale[:, g, P * c : P * (c + 1)],
+                        rhs=x_codes[:, s, P * g : P * (g + 1)].bitcast(FP8X4),
+                        rhs_scale=x_scale[:, s, P * g : P * (g + 1)],
+                        start=(g == 0),
+                        stop=(g == G1 - 1),
+                    )
+            cqg = work.tile([P, P, 4], BF16, name="cqg%d" % s, tag="cqg", bufs=2, align_bytes=64)
+            nc.scalar.copy(out=cqg[:], in_=cqp[:].rearrange("p c t -> p t c"))
+            cq_grouped[s] = cqg
+
+        def quant_cq(s):
+            nc.vector.quantize_mx(
+                out=cq_codes[:, s, :].bitcast(FP8X4),
+                scales=cq_scale[:, s, :],
+                in_=cq_grouped[s][:].rearrange("p t c -> p (t c)"),
+            )
+
+        def token_tiles(first, last):
+            for i in range(first, last + 3):
+                if i < last:
+                    transpose_x(i)
+                if first <= i - 1 < last:
+                    quant_x(i - 1)
+                if first <= i - 2 < last:
+                    first_matmul(i - 2)
+                    quant_cq(i - 2)
+
+        def prepare_wb(g):
+            for kind in range(2):
+                wbg = work.tile([P, 512, 4], BF16, name="wbg", tag="wbg", bufs=3, align_bytes=64)
+                src = wb_raw[g][:].rearrange("p t (h k c) -> p k h c t", h=HG, k=2)
+                nc.scalar.copy(out=wbg[:].rearrange("p (h c) t -> p h c t", h=HG), in_=src[:, kind])
+                nc.vector.quantize_mx(
+                    out=wb_codes[:, g, kind, :].bitcast(FP8X4),
+                    scales=wb_scale[:, g, kind, :],
+                    in_=wbg[:].rearrange("p c t -> p (c t)"),
+                )
+
+        out_view = out.rearrange("b h (q s) f -> b q h s f", s=S)
+
+        def unit(g, sh):
+            res = work.tile([P, HG, 4, QH], F32, name="res", tag="big16", bufs=3)
+            for pair in range(2):
+                part = work.tile([P, HG, 2, ROPE], F32, name="part", tag="part", bufs=3)
+                for k in range(2):
+                    sl = 2 * pair + k
+                    s = 4 * sh + sl
+                    banks = []
+                    for kind in range(2):
+                        q_ps = psum.tile([P, 512], F32, name="q_ps", tag="ps")
+                        nc.tensor.matmul_mx(
+                            out=q_ps[:],
+                            lhsT=cq_codes[:, s, :].bitcast(FP8X4),
+                            lhsT_scale=cq_scale[:, s, :],
+                            rhs=wb_codes[:, g, kind, :].bitcast(FP8X4),
+                            rhs_scale=wb_scale[:, g, kind, :],
+                            start=True,
+                            stop=True,
+                        )
+                        banks.append(q_ps)
+                    nc.scalar.copy(
+                        out=res[:, :, sl, 0:NOPE], in_=banks[0][:].rearrange("p (h c) -> p h c", h=HG)
+                    )
+                    pairs = banks[1][:].rearrange("p (h m e) -> p h m e", h=HG, e=2)
+                    shape = [P, HG, FREQ, 2]
+                    nc.vector.tensor_tensor(
+                        out=res[:, :, sl, NOPE:QH].rearrange("p h (m e) -> p h m e", e=2),
+                        in0=pairs[:, :, :, 0:1].to_broadcast(shape),
+                        in1=cos_sin[:, s].unsqueeze(1).to_broadcast(shape),
+                        op=ALU.mult,
+                    )
+                    nc.vector.tensor_tensor(
+                        out=part[:, :, k, :].rearrange("p h (m e) -> p h m e", e=2),
+                        in0=pairs[:, :, :, 1:2].to_broadcast(shape),
+                        in1=nsin_cos[:, s].unsqueeze(1).to_broadcast(shape),
+                        op=ALU.mult,
+                    )
+                nc.gpsimd.tensor_tensor(
+                    out=res[:, :, 2 * pair : 2 * pair + 2, NOPE:QH],
+                    in0=res[:, :, 2 * pair : 2 * pair + 2, NOPE:QH],
+                    in1=part[:],
+                    op=ALU.add,
+                )
+            for b in range(B):
+                nc.sync.dma_start(
+                    out=out_view[b, :, HG * g : HG * (g + 1), 4 * sh : 4 * sh + 4, :], in_=res[b::4]
+                )
+
+        token_tiles(0, 4)
+        prepare_wb(0)
+        token_tiles(4, 8)
+        for g in range(NG):
+            unit(g, 0)
+            if g + 1 < NG:
+                prepare_wb(g + 1)
+            unit(g, 1)

@@ -34,8 +34,16 @@ def tile_multilatentattention_pa_kernel(tc, x, Wqa, Wqb, out):
         work = ctx.enter_context(tc.tile_pool(name="work", bufs=2))
         psum = ctx.enter_context(tc.psum_pool(name="psum", bufs=8))
 
+        warm = keep.tile([P, 1], F32, name="warm")
+        nc.vector.memset(warm[:], 0.0)
+        nc.scalar.activation(out=warm[:], in_=warm[:], func=ACT.Sin)
+
         ident = keep.tile([P, P], F32, name="ident")
         masks.make_identity(nc, ident[:])
+        perm = keep.tile([P, P], F32, name="perm")
+        nc.vector.tensor_copy(
+            out=perm[:].rearrange("p (q b) -> p q b", b=B), in_=ident[:].rearrange("p (b q) -> p q b", b=B)
+        )
 
         two_p = keep.tile([P, S], I32, name="two_p")
         nc.gpsimd.iota(two_p[:], pattern=[[0, S]], base=0, channel_multiplier=2)
@@ -57,80 +65,68 @@ def tile_multilatentattention_pa_kernel(tc, x, Wqa, Wqb, out):
                 out=theta[:, w : 2 * w], in0=theta[:, 0:w], scalar1=BASE ** (-2.0 * w / ROPE)
             )
 
-        turns = keep.tile([P, S, FREQ], F32, name="turns")
-        nc.gpsimd.tensor_tensor(
-            out=turns[:],
+        scratch = work.tile([P, 6, S * FREQ], F32, name="scratch", tag="res", bufs=4)
+        turns = scratch[:, 0, :]
+        nc.vector.tensor_tensor(
+            out=turns.rearrange("p (s m) -> p s m", s=S),
             in0=theta[:].unsqueeze(1).to_broadcast([P, S, FREQ]),
             in1=pos_a[:].unsqueeze(2).to_broadcast([P, S, FREQ]),
             op=ALU.mult,
         )
-        whole_i = keep.tile([P, S, FREQ], I32, name="whole_i")
-        nc.vector.tensor_copy(out=whole_i[:], in_=turns[:])
-        whole_f = keep.tile([P, S, FREQ], F32, name="whole_f")
-        nc.vector.tensor_copy(out=whole_f[:], in_=whole_i[:])
-        nc.gpsimd.tensor_tensor(out=turns[:], in0=turns[:], in1=whole_f[:], op=ALU.subtract)
-        turns_c = keep.tile([P, S, FREQ], F32, name="turns_c")
-        nc.gpsimd.tensor_scalar(
-            out=turns_c[:], in0=turns[:], scalar1=1.0, scalar2=0.25, op0=ALU.mult, op1=ALU.add
-        )
-        planes = keep.tile([P, 3, S * FREQ], F32, name="planes")
+        whole_i = scratch[:, 1, :].bitcast(I32)
+        nc.vector.tensor_copy(out=whole_i, in_=turns)
+        whole_f = scratch[:, 2, :]
+        nc.vector.tensor_copy(out=whole_f, in_=whole_i)
+        nc.vector.tensor_tensor(out=turns, in0=turns, in1=whole_f, op=ALU.subtract)
+        turns_c = scratch[:, 3, :]
+        nc.vector.tensor_scalar_add(out=turns_c, in0=turns, scalar1=0.25)
+        fold_s = scratch[:, 4, :]
         nc.vector.scalar_tensor_tensor(
-            out=planes[:, 2, :],
-            in0=turns[:].rearrange("p s m -> p (s m)"),
-            scalar=0.5,
-            in1=turns[:].rearrange("p s m -> p (s m)"),
-            op0=ALU.is_gt,
-            op1=ALU.subtract,
+            out=fold_s, in0=turns, scalar=0.5, in1=turns, op0=ALU.is_gt, op1=ALU.subtract
         )
+        fold_c = scratch[:, 5, :]
         nc.vector.scalar_tensor_tensor(
-            out=planes[:, 1, :],
-            in0=turns_c[:].rearrange("p s m -> p (s m)"),
-            scalar=0.5,
-            in1=turns_c[:].rearrange("p s m -> p (s m)"),
-            op0=ALU.is_gt,
-            op1=ALU.subtract,
+            out=fold_c, in0=turns_c, scalar=0.5, in1=turns_c, op0=ALU.is_gt, op1=ALU.subtract
         )
-        nc.gpsimd.tensor_scalar(
-            out=planes[:, 0, :], in0=planes[:, 2, :], scalar1=-1.0, scalar2=0.0, op0=ALU.mult, op1=ALU.add
-        )
-        cos_sin = keep.tile([P, S, FREQ, 2], F32, name="cos_sin")
-        nsin_cos = keep.tile([P, S, FREQ, 2], F32, name="nsin_cos")
+        table = keep.tile([P, 3, S, FREQ], F32, name="table")
         nc.scalar.activation(
-            out=cos_sin[:].rearrange("p s m e -> p (s m) e"),
-            in_=planes[:, 1:3, :].rearrange("p e x -> p x e"),
-            func=ACT.Sin,
-            scale=-2.0 * math.pi,
+            out=table[:, 2].rearrange("p s m -> p (s m)"), in_=fold_s, func=ACT.Sin, scale=-2.0 * math.pi
         )
         nc.scalar.activation(
-            out=nsin_cos[:].rearrange("p s m e -> p (s m) e"),
-            in_=planes[:, 0:2, :].rearrange("p e x -> p x e"),
-            func=ACT.Sin,
-            scale=-2.0 * math.pi,
+            out=table[:, 0].rearrange("p s m -> p (s m)"), in_=fold_s, func=ACT.Sin, scale=2.0 * math.pi
+        )
+        nc.scalar.activation(
+            out=table[:, 1].rearrange("p s m -> p (s m)"), in_=fold_c, func=ACT.Sin, scale=-2.0 * math.pi
         )
 
-        wa_codes = keep.tile([P, G1, QR], U32, name="wa_codes", align_bytes=64)
-        wa_scale = keep.tile([P, G1, QR], U8, name="wa_scale", align_bytes=64)
-        x_codes = keep.tile([P, S, G1 * P], U32, name="x_codes", align_bytes=64)
-        x_scale = keep.tile([P, S, G1 * P], U8, name="x_scale", align_bytes=64)
-        cq_codes = keep.tile([P, S, P], U32, name="cq_codes", align_bytes=64)
-        cq_scale = keep.tile([P, S, P], U8, name="cq_scale", align_bytes=64)
-        wb_codes = keep.tile([P, NG, 2, 512], U32, name="wb_codes", align_bytes=64)
-        wb_scale = keep.tile([P, NG, 2, 512], U8, name="wb_scale", align_bytes=64)
+        wa_codes = [keep.tile([P, QR], U32, name="wa_codes%d" % g, align_bytes=64) for g in range(G1)]
+        wa_scale = [keep.tile([P, QR], U8, name="wa_scale%d" % g, align_bytes=64) for g in range(G1)]
+        x_codes = [keep.tile([P, G1 * P], U32, name="x_codes%d" % s, align_bytes=64) for s in range(S)]
+        x_scale = [keep.tile([P, G1 * P], U8, name="x_scale%d" % s, align_bytes=64) for s in range(S)]
+        cq_codes = [keep.tile([P, P], U32, name="cq_codes%d" % s, align_bytes=64) for s in range(S)]
+        cq_scale = [keep.tile([P, P], U8, name="cq_scale%d" % s, align_bytes=64) for s in range(S)]
+        wb_codes = [keep.tile([P, 512], U32, name="wb_codes%d" % i, align_bytes=64) for i in range(2 * NG)]
+        wb_scale = [keep.tile([P, 512], U8, name="wb_scale%d" % i, align_bytes=64) for i in range(2 * NG)]
 
-        wa_raw = work.tile([P, G1, 2, 1024], BF16, name="wa_raw", tag="big16", bufs=3)
-        for g in range(G1):
-            nc.sync.dma_start(
-                out=wa_raw[:, g],
-                in_=Wqa[512 * g : 512 * (g + 1), :].rearrange("(u p e) c -> p u (e c)", u=2, e=2),
-            )
-        x_view = x.rearrange("b (q s) k -> b q s k", s=S)
+        wa_raw = []
+
+        def load_wa(half):
+            wa = work.tile([P, 2, 2, 1024], BF16, name="wa_raw%d" % half, tag="raw8", bufs=6)
+            for gg in range(2):
+                g = 2 * half + gg
+                nc.sync.dma_start(
+                    out=wa[:, gg],
+                    in_=Wqa[512 * g : 512 * (g + 1), :].rearrange("(u p e) c -> p u (e c)", u=2, e=2),
+                )
+            wa_raw.append(wa)
+
+        x_view = x.flatten_outer_dims().rearrange("(p s) k -> p s k", s=S)
         x_raw = []
         wb_raw = []
 
         def load_x(sq):
             xs = work.tile([P, 2, E], BF16, name="x_raw%d" % sq, tag="raw8", bufs=6)
-            for b in range(B):
-                nc.sync.dma_start(out=xs[b::4, :, :], in_=x_view[b, :, 2 * sq : 2 * sq + 2, :])
+            nc.sync.dma_start(out=xs[:], in_=x_view[:, 2 * sq : 2 * sq + 2, :])
             x_raw.append(xs)
 
         def load_wb(g):
@@ -141,11 +137,13 @@ def tile_multilatentattention_pa_kernel(tc, x, Wqa, Wqb, out):
             wb_raw.append(wb)
 
         load_x(0)
-        load_x(1)
         load_wb(0)
+        load_wa(0)
+        load_wa(1)
+        load_x(1)
+        load_wb(1)
         load_x(2)
         load_x(3)
-        load_wb(1)
         load_wb(2)
         load_wb(3)
 
@@ -153,7 +151,7 @@ def tile_multilatentattention_pa_kernel(tc, x, Wqa, Wqb, out):
 
         def wa_regroup(g):
             wag = work.tile([P, QR, 4], BF16, name="wag%d" % g, tag="wag", bufs=2, align_bytes=64)
-            src = wa_raw[:, g].rearrange("p u (e c) -> p (u e) c", e=2)
+            src = wa_raw[g // 2][:, g % 2].rearrange("p u (e c) -> p (u e) c", e=2)
             nc.vector.tensor_copy(
                 out=wag[:].rearrange("p (c i) t -> p c t i", i=4),
                 in_=src.rearrange("p t (c i) -> p c t i", i=4),
@@ -162,21 +160,22 @@ def tile_multilatentattention_pa_kernel(tc, x, Wqa, Wqb, out):
 
         def wa_quant(g):
             nc.vector.quantize_mx(
-                out=wa_codes[:, g, :].bitcast(FP8X4),
-                scales=wa_scale[:, g, :],
+                out=wa_codes[g][:].bitcast(FP8X4),
+                scales=wa_scale[g][:],
                 in_=wa_grouped[g][:].rearrange("p c t -> p (c t)"),
             )
 
-        wa_regroup(0)
-        for g in range(1, G1):
-            wa_regroup(g)
-            wa_quant(g - 1)
-        wa_quant(G1 - 1)
+        def prepare_wa():
+            wa_regroup(0)
+            for g in range(1, G1):
+                wa_regroup(g)
+                wa_quant(g - 1)
+            wa_quant(G1 - 1)
 
         x_grouped = {}
         cq_grouped = {}
 
-        def transpose_x(s):
+        def transpose_x(s, copy):
             words = x_raw[s // 2][:].bitcast(F32)
             xg = work.tile([P, G1, P, 4], BF16, name="xg%d" % s, tag="xg", bufs=3, align_bytes=64)
             xg_words = xg[:].bitcast(F32)
@@ -186,9 +185,9 @@ def tile_multilatentattention_pa_kernel(tc, x, Wqa, Wqb, out):
                     for u in range(2):
                         col = 256 * (2 * half + gg) + 128 * u
                         nc.tensor.transpose(
-                            out=xt[:, gg, u, :], in_=words[:, s % 2, col : col + P], identity=ident[:]
+                            out=xt[:, gg, u, :], in_=words[:, s % 2, col : col + P], identity=perm[:]
                         )
-                nc.scalar.copy(
+                copy(
                     out=xg_words[:, 2 * half : 2 * half + 2, :, :],
                     in_=xt[:].rearrange("p g u t -> p g t u"),
                 )
@@ -196,8 +195,8 @@ def tile_multilatentattention_pa_kernel(tc, x, Wqa, Wqb, out):
 
         def quant_x(s):
             nc.vector.quantize_mx(
-                out=x_codes[:, s, :].bitcast(FP8X4),
-                scales=x_scale[:, s, :],
+                out=x_codes[s][:].bitcast(FP8X4),
+                scales=x_scale[s][:],
                 in_=x_grouped[s][:].rearrange("p g t j -> p (g t j)"),
             )
 
@@ -207,10 +206,10 @@ def tile_multilatentattention_pa_kernel(tc, x, Wqa, Wqb, out):
                 for g in range(G1):
                     nc.tensor.matmul_mx(
                         out=cqp[:, c, :],
-                        lhsT=wa_codes[:, g, P * c : P * (c + 1)].bitcast(FP8X4),
-                        lhsT_scale=wa_scale[:, g, P * c : P * (c + 1)],
-                        rhs=x_codes[:, s, P * g : P * (g + 1)].bitcast(FP8X4),
-                        rhs_scale=x_scale[:, s, P * g : P * (g + 1)],
+                        lhsT=wa_codes[g][:, P * c : P * (c + 1)].bitcast(FP8X4),
+                        lhsT_scale=wa_scale[g][:, P * c : P * (c + 1)],
+                        rhs=x_codes[s][:, P * g : P * (g + 1)].bitcast(FP8X4),
+                        rhs_scale=x_scale[s][:, P * g : P * (g + 1)],
                         start=(g == 0),
                         stop=(g == G1 - 1),
                     )
@@ -220,87 +219,134 @@ def tile_multilatentattention_pa_kernel(tc, x, Wqa, Wqb, out):
 
         def quant_cq(s):
             nc.vector.quantize_mx(
-                out=cq_codes[:, s, :].bitcast(FP8X4),
-                scales=cq_scale[:, s, :],
+                out=cq_codes[s][:].bitcast(FP8X4),
+                scales=cq_scale[s][:],
                 in_=cq_grouped[s][:].rearrange("p t c -> p (t c)"),
             )
 
-        def token_tiles(first, last):
-            for i in range(first, last + 3):
-                if i < last:
-                    transpose_x(i)
-                if first <= i - 1 < last:
-                    quant_x(i - 1)
-                if first <= i - 2 < last:
-                    first_matmul(i - 2)
-                    quant_cq(i - 2)
-
-        def prepare_wb(g):
-            for kind in range(2):
-                wbg = work.tile([P, 512, 4], BF16, name="wbg", tag="wbg", bufs=3, align_bytes=64)
-                src = wb_raw[g][:].rearrange("p t (h k c) -> p k h c t", h=HG, k=2)
-                nc.scalar.copy(out=wbg[:].rearrange("p (h c) t -> p h c t", h=HG), in_=src[:, kind])
-                nc.vector.quantize_mx(
-                    out=wb_codes[:, g, kind, :].bitcast(FP8X4),
-                    scales=wb_scale[:, g, kind, :],
-                    in_=wbg[:].rearrange("p c t -> p (c t)"),
-                )
+        def prepare_wb(g, kind, copy):
+            wbg = work.tile([P, 512, 4], BF16, name="wbg", tag="wbg", bufs=2, align_bytes=64)
+            src = wb_raw[g][:].rearrange("p t (h k c) -> p k h c t", h=HG, k=2)
+            copy(out=wbg[:].rearrange("p (h c) t -> p h c t", h=HG), in_=src[:, kind])
+            nc.vector.quantize_mx(
+                out=wb_codes[2 * g + kind][:].bitcast(FP8X4),
+                scales=wb_scale[2 * g + kind][:],
+                in_=wbg[:].rearrange("p c t -> p (c t)"),
+            )
 
         out_view = out.rearrange("b h (q s) f -> b q h s f", s=S)
 
-        def unit(g, sh):
-            res = work.tile([P, HG, 4, QH], F32, name="res", tag="big16", bufs=3)
-            for pair in range(2):
-                part = work.tile([P, HG, 2, ROPE], F32, name="part", tag="part", bufs=3)
-                for k in range(2):
-                    sl = 2 * pair + k
-                    s = 4 * sh + sl
-                    banks = []
-                    for kind in range(2):
-                        q_ps = psum.tile([P, 512], F32, name="q_ps", tag="ps")
-                        nc.tensor.matmul_mx(
-                            out=q_ps[:],
-                            lhsT=cq_codes[:, s, :].bitcast(FP8X4),
-                            lhsT_scale=cq_scale[:, s, :],
-                            rhs=wb_codes[:, g, kind, :].bitcast(FP8X4),
-                            rhs_scale=wb_scale[:, g, kind, :],
-                            start=True,
-                            stop=True,
-                        )
-                        banks.append(q_ps)
-                    nc.scalar.copy(
-                        out=res[:, :, sl, 0:NOPE], in_=banks[0][:].rearrange("p (h c) -> p h c", h=HG)
-                    )
-                    pairs = banks[1][:].rearrange("p (h m e) -> p h m e", h=HG, e=2)
-                    shape = [P, HG, FREQ, 2]
-                    nc.vector.tensor_tensor(
-                        out=res[:, :, sl, NOPE:QH].rearrange("p h (m e) -> p h m e", e=2),
-                        in0=pairs[:, :, :, 0:1].to_broadcast(shape),
-                        in1=cos_sin[:, s].unsqueeze(1).to_broadcast(shape),
-                        op=ALU.mult,
-                    )
-                    nc.vector.tensor_tensor(
-                        out=part[:, :, k, :].rearrange("p h (m e) -> p h m e", e=2),
-                        in0=pairs[:, :, :, 1:2].to_broadcast(shape),
-                        in1=nsin_cos[:, s].unsqueeze(1).to_broadcast(shape),
-                        op=ALU.mult,
-                    )
-                nc.gpsimd.tensor_tensor(
-                    out=res[:, :, 2 * pair : 2 * pair + 2, NOPE:QH],
-                    in0=res[:, :, 2 * pair : 2 * pair + 2, NOPE:QH],
-                    in1=part[:],
-                    op=ALU.add,
+        def second_matmul(g, kind, s):
+            q_ps = psum.tile([P, 512], F32, name="q_ps", tag="ps")
+            nc.tensor.matmul_mx(
+                out=q_ps[:],
+                lhsT=cq_codes[s][:].bitcast(FP8X4),
+                lhsT_scale=cq_scale[s][:],
+                rhs=wb_codes[2 * g + kind][:].bitcast(FP8X4),
+                rhs_scale=wb_scale[2 * g + kind][:],
+                start=True,
+                stop=True,
+            )
+            return q_ps
+
+        results = {}
+
+        def nope_part(g, s):
+            if s % 4 == 0:
+                results[g] = work.tile([P, HG, 4, QH], F32, name="res", tag="res", bufs=4)
+            q_nope = second_matmul(g, 0, s)
+            nc.scalar.copy(
+                out=results[g][:, :, s % 4, 0:NOPE], in_=q_nope[:].rearrange("p (h c) -> p h c", h=HG)
+            )
+
+        def rope_part(g, s0):
+            shape = [P, HG, FREQ, 2]
+            part_a = work.tile([P, HG, 2, ROPE], F32, name="part_a", tag="part_a", bufs=3)
+            part_b = work.tile([P, HG, 2, ROPE], F32, name="part_b", tag="part_b", bufs=3)
+            for k in range(2):
+                s = s0 + k
+                q_rope = second_matmul(g, 1, s)
+                pairs = q_rope[:].rearrange("p (h m e) -> p h m e", h=HG, e=2)
+                nc.vector.tensor_tensor(
+                    out=part_a[:, :, k, :].rearrange("p h (m e) -> p h m e", e=2),
+                    in0=pairs[:, :, :, 0:1].to_broadcast(shape),
+                    in1=table[:, 1:3, s, :].rearrange("p e m -> p m e").unsqueeze(1).to_broadcast(shape),
+                    op=ALU.mult,
                 )
+                nc.vector.tensor_tensor(
+                    out=part_b[:, :, k, :].rearrange("p h (m e) -> p h m e", e=2),
+                    in0=pairs[:, :, :, 1:2].to_broadcast(shape),
+                    in1=table[:, 0:2, s, :].rearrange("p e m -> p m e").unsqueeze(1).to_broadcast(shape),
+                    op=ALU.mult,
+                )
+            nc.gpsimd.tensor_tensor(
+                out=results[g][:, :, s0 % 4 : s0 % 4 + 2, NOPE:QH], in0=part_a[:], in1=part_b[:], op=ALU.add
+            )
+
+        def store(g, s0, count):
             for b in range(B):
                 nc.sync.dma_start(
-                    out=out_view[b, :, HG * g : HG * (g + 1), 4 * sh : 4 * sh + 4, :], in_=res[b::4]
+                    out=out_view[b, :, HG * g : HG * (g + 1), s0 : s0 + count, :],
+                    in_=results[g][b::4, :, s0 % 4 : s0 % 4 + count, :],
                 )
 
-        token_tiles(0, 4)
-        prepare_wb(0)
-        token_tiles(4, 8)
-        for g in range(NG):
-            unit(g, 0)
-            if g + 1 < NG:
-                prepare_wb(g + 1)
-            unit(g, 1)
+        def tiles_in(s0, copy):
+            transpose_x(s0, copy)
+            transpose_x(s0 + 1, copy)
+            quant_x(s0)
+            quant_x(s0 + 1)
+
+        def tiles_through(s0):
+            first_matmul(s0)
+            first_matmul(s0 + 1)
+            quant_cq(s0)
+            quant_cq(s0 + 1)
+
+        def cells(g, s0):
+            nope_part(g, s0)
+            nope_part(g, s0 + 1)
+            rope_part(g, s0)
+            if s0 % 4 == 2:
+                store(g, s0 - 2, 4)
+
+        by_scalar = nc.scalar.copy
+        by_vector = nc.vector.tensor_copy
+        tiles_in(0, by_scalar)
+        prepare_wb(0, 1, by_scalar)
+        prepare_wb(0, 0, by_scalar)
+        prepare_wa()
+        tiles_through(0)
+        tiles_in(2, by_scalar)
+        cells(0, 0)
+        prepare_wb(1, 1, by_vector)
+        prepare_wb(1, 0, by_scalar)
+        cells(1, 0)
+        tiles_through(2)
+        tiles_in(4, by_scalar)
+        cells(0, 2)
+        cells(1, 2)
+        tiles_through(4)
+        tiles_in(6, by_scalar)
+        cells(0, 4)
+        prepare_wb(2, 1, by_scalar)
+        cells(1, 4)
+        tiles_through(6)
+        cells(0, 6)
+        prepare_wb(2, 0, by_scalar)
+        cells(1, 6)
+        for g in range(2, NG):
+            for sh in range(2):
+                for sl in range(4):
+                    nope_part(g, 4 * sh + sl)
+                if g + 1 < NG and sh == 0:
+                    prepare_wb(g + 1, 1, by_scalar)
+                    prepare_wb(g + 1, 0, by_scalar)
+                last = g == NG - 1 and sh == 1
+                rope_part(g, 4 * sh)
+                if last:
+                    store(g, 4 * sh, 2)
+                rope_part(g, 4 * sh + 2)
+                if last:
+                    store(g, 4 * sh + 2, 2)
+                else:
+                    store(g, 4 * sh, 4)

@@ -33,71 +33,7 @@ def tile_multilatentattention_pa_kernel(tc, x, Wqa, Wqb, out):
         keep = ctx.enter_context(tc.tile_pool(name="keep", bufs=1))
         work = ctx.enter_context(tc.tile_pool(name="work", bufs=2))
         psum = ctx.enter_context(tc.psum_pool(name="psum", bufs=8))
-
-        warm = keep.tile([P, 1], F32, name="warm")
-        nc.vector.memset(warm[:], 0.0)
-        nc.scalar.activation(out=warm[:], in_=warm[:], func=ACT.Sin)
-
-        ident = keep.tile([P, P], F32, name="ident")
-        masks.make_identity(nc, ident[:])
-        perm = keep.tile([P, P], F32, name="perm")
-        nc.vector.tensor_copy(
-            out=perm[:].rearrange("p (q b) -> p q b", b=B), in_=ident[:].rearrange("p (b q) -> p q b", b=B)
-        )
-
-        two_p = keep.tile([P, S], I32, name="two_p")
-        nc.gpsimd.iota(two_p[:], pattern=[[0, S]], base=0, channel_multiplier=2)
-        s_idx = keep.tile([P, S], I32, name="s_idx")
-        nc.gpsimd.iota(s_idx[:], pattern=[[1, S]], base=0, channel_multiplier=0)
-        nc.vector.tensor_single_scalar(out=two_p[:], in_=two_p[:], scalar=248, op=ALU.bitwise_and)
-        pos_a = keep.tile([P, S], F32, name="pos_a")
-        nc.vector.tensor_copy(out=pos_a[:], in_=two_p[:])
-        pos_b = keep.tile([P, S], F32, name="pos_b")
-        nc.vector.tensor_copy(out=pos_b[:], in_=s_idx[:])
-        nc.vector.tensor_tensor(out=pos_a[:], in0=pos_a[:], in1=pos_b[:], op=ALU.add)
-        nc.vector.tensor_scalar_mul(out=pos_a[:], in0=pos_a[:], scalar1=1.0 / (2.0 * math.pi))
-
-        theta = keep.tile([P, FREQ], F32, name="theta")
-        nc.vector.memset(theta[:, 0:1], 1.0)
-        for j in range(6):
-            w = 1 << j
-            nc.vector.tensor_scalar_mul(
-                out=theta[:, w : 2 * w], in0=theta[:, 0:w], scalar1=BASE ** (-2.0 * w / ROPE)
-            )
-
-        scratch = work.tile([P, 6, S * FREQ], F32, name="scratch", tag="res", bufs=4)
-        turns = scratch[:, 0, :]
-        nc.vector.tensor_tensor(
-            out=turns.rearrange("p (s m) -> p s m", s=S),
-            in0=theta[:].unsqueeze(1).to_broadcast([P, S, FREQ]),
-            in1=pos_a[:].unsqueeze(2).to_broadcast([P, S, FREQ]),
-            op=ALU.mult,
-        )
-        whole_i = scratch[:, 1, :].bitcast(I32)
-        nc.vector.tensor_copy(out=whole_i, in_=turns)
-        whole_f = scratch[:, 2, :]
-        nc.vector.tensor_copy(out=whole_f, in_=whole_i)
-        nc.vector.tensor_tensor(out=turns, in0=turns, in1=whole_f, op=ALU.subtract)
-        turns_c = scratch[:, 3, :]
-        nc.vector.tensor_scalar_add(out=turns_c, in0=turns, scalar1=0.25)
-        fold_s = scratch[:, 4, :]
-        nc.vector.scalar_tensor_tensor(
-            out=fold_s, in0=turns, scalar=0.5, in1=turns, op0=ALU.is_gt, op1=ALU.subtract
-        )
-        fold_c = scratch[:, 5, :]
-        nc.vector.scalar_tensor_tensor(
-            out=fold_c, in0=turns_c, scalar=0.5, in1=turns_c, op0=ALU.is_gt, op1=ALU.subtract
-        )
-        table = keep.tile([P, 3, S, FREQ], F32, name="table")
-        nc.scalar.activation(
-            out=table[:, 2].rearrange("p s m -> p (s m)"), in_=fold_s, func=ACT.Sin, scale=-2.0 * math.pi
-        )
-        nc.scalar.activation(
-            out=table[:, 0].rearrange("p s m -> p (s m)"), in_=fold_s, func=ACT.Sin, scale=2.0 * math.pi
-        )
-        nc.scalar.activation(
-            out=table[:, 1].rearrange("p s m -> p (s m)"), in_=fold_c, func=ACT.Sin, scale=-2.0 * math.pi
-        )
+        ctx.enter_context(tc.manual_schedule())
 
         wa_codes = [keep.tile([P, QR], U32, name="wa_codes%d" % g, align_bytes=64) for g in range(G1)]
         wa_scale = [keep.tile([P, QR], U8, name="wa_scale%d" % g, align_bytes=64) for g in range(G1)]
@@ -109,6 +45,9 @@ def tile_multilatentattention_pa_kernel(tc, x, Wqa, Wqb, out):
         wb_scale = [keep.tile([P, 512], U8, name="wb_scale%d" % i, align_bytes=64) for i in range(2 * NG)]
 
         wa_raw = []
+        x_raw = []
+        wb_raw = []
+        x_view = x.flatten_outer_dims().rearrange("(p s) k -> p s k", s=S)
 
         def load_wa(half):
             wa = work.tile([P, 2, 2, 1024], BF16, name="wa_raw%d" % half, tag="raw8", bufs=6)
@@ -120,13 +59,14 @@ def tile_multilatentattention_pa_kernel(tc, x, Wqa, Wqb, out):
                 )
             wa_raw.append(wa)
 
-        x_view = x.flatten_outer_dims().rearrange("(p s) k -> p s k", s=S)
-        x_raw = []
-        wb_raw = []
-
-        def load_x(sq):
+        def load_x(sq, pieces):
             xs = work.tile([P, 2, E], BF16, name="x_raw%d" % sq, tag="raw8", bufs=6)
-            nc.sync.dma_start(out=xs[:], in_=x_view[:, 2 * sq : 2 * sq + 2, :])
+            step = 2 // pieces
+            for i in range(pieces):
+                nc.sync.dma_start(
+                    out=xs[:, step * i : step * (i + 1), :],
+                    in_=x_view[:, 2 * sq + step * i : 2 * sq + step * (i + 1), :],
+                )
             x_raw.append(xs)
 
         def load_wb(g):
@@ -136,16 +76,79 @@ def tile_multilatentattention_pa_kernel(tc, x, Wqa, Wqb, out):
             )
             wb_raw.append(wb)
 
-        load_x(0)
-        load_wb(0)
         load_wa(0)
         load_wa(1)
-        load_x(1)
+        load_x(0, 2)
+        load_x(1, 1)
+        load_x(2, 1)
+        load_wb(0)
+        load_x(3, 1)
         load_wb(1)
-        load_x(2)
-        load_x(3)
         load_wb(2)
         load_wb(3)
+
+        warm = keep.tile([P, 1], F32, name="warm")
+        nc.vector.memset(warm[:], 0.0)
+        nc.scalar.activation(out=warm[:], in_=warm[:], func=ACT.Sin)
+
+        ident = keep.tile([P, P], F32, name="ident")
+        masks.make_identity(nc, ident[:])
+        two_p = keep.tile([P, S], I32, name="two_p")
+        nc.gpsimd.iota(two_p[:], pattern=[[0, S]], base=0, channel_multiplier=2)
+        s_idx = keep.tile([P, S], I32, name="s_idx")
+        nc.gpsimd.iota(s_idx[:], pattern=[[1, S]], base=0, channel_multiplier=0)
+
+        perm = keep.tile([P, P], F32, name="perm")
+        nc.vector.tensor_copy(
+            out=perm[:].rearrange("p (q b) -> p q b", b=B), in_=ident[:].rearrange("p (b q) -> p q b", b=B)
+        )
+        nc.vector.tensor_single_scalar(out=two_p[:], in_=two_p[:], scalar=248, op=ALU.bitwise_and)
+        pos_a = keep.tile([P, S], F32, name="pos_a")
+        nc.vector.tensor_copy(out=pos_a[:], in_=two_p[:])
+        pos_b = keep.tile([P, S], F32, name="pos_b")
+        nc.vector.tensor_copy(out=pos_b[:], in_=s_idx[:])
+        nc.vector.tensor_tensor(out=pos_a[:], in0=pos_a[:], in1=pos_b[:], op=ALU.add)
+        nc.vector.tensor_scalar_mul(out=pos_a[:], in0=pos_a[:], scalar1=1.0 / (2.0 * math.pi))
+        theta = keep.tile([P, FREQ], F32, name="theta")
+        nc.vector.memset(theta[:, 0:1], 1.0)
+        for j in range(6):
+            w = 1 << j
+            nc.vector.tensor_scalar_mul(
+                out=theta[:, w : 2 * w], in0=theta[:, 0:w], scalar1=BASE ** (-2.0 * w / ROPE)
+            )
+        scratch = work.tile([P, 6, S * FREQ], F32, name="scratch", tag="res", bufs=3)
+        turns = scratch[:, 0, :]
+        whole_i = scratch[:, 1, :].bitcast(I32)
+        whole_f = scratch[:, 2, :]
+        turns_c = scratch[:, 3, :]
+        fold_s = scratch[:, 4, :]
+        fold_c = scratch[:, 5, :]
+        table = keep.tile([P, 3, S, FREQ], F32, name="table")
+        nc.vector.tensor_tensor(
+            out=turns.rearrange("p (s m) -> p s m", s=S),
+            in0=theta[:].unsqueeze(1).to_broadcast([P, S, FREQ]),
+            in1=pos_a[:].unsqueeze(2).to_broadcast([P, S, FREQ]),
+            op=ALU.mult,
+        )
+        nc.vector.tensor_copy(out=whole_i, in_=turns)
+        nc.vector.tensor_copy(out=whole_f, in_=whole_i)
+
+        def finish_tables():
+            nc.vector.tensor_tensor(out=turns, in0=turns, in1=whole_f, op=ALU.subtract)
+            nc.vector.tensor_scalar_add(out=turns_c, in0=turns, scalar1=0.25)
+            nc.vector.scalar_tensor_tensor(
+                out=fold_s, in0=turns, scalar=0.5, in1=turns, op0=ALU.is_gt, op1=ALU.subtract
+            )
+            nc.vector.scalar_tensor_tensor(
+                out=fold_c, in0=turns_c, scalar=0.5, in1=turns_c, op0=ALU.is_gt, op1=ALU.subtract
+            )
+            for plane, src, sign in ((2, fold_s, -1.0), (0, fold_s, 1.0), (1, fold_c, -1.0)):
+                nc.scalar.activation(
+                    out=table[:, plane].rearrange("p s m -> p (s m)"),
+                    in_=src,
+                    func=ACT.Sin,
+                    scale=sign * 2.0 * math.pi,
+                )
 
         wa_grouped = []
 
@@ -165,17 +168,10 @@ def tile_multilatentattention_pa_kernel(tc, x, Wqa, Wqb, out):
                 in_=wa_grouped[g][:].rearrange("p c t -> p (c t)"),
             )
 
-        def prepare_wa():
-            wa_regroup(0)
-            for g in range(1, G1):
-                wa_regroup(g)
-                wa_quant(g - 1)
-            wa_quant(G1 - 1)
-
         x_grouped = {}
         cq_grouped = {}
 
-        def transpose_x(s, copy):
+        def transpose_x(s):
             words = x_raw[s // 2][:].bitcast(F32)
             xg = work.tile([P, G1, P, 4], BF16, name="xg%d" % s, tag="xg", bufs=3, align_bytes=64)
             xg_words = xg[:].bitcast(F32)
@@ -187,7 +183,7 @@ def tile_multilatentattention_pa_kernel(tc, x, Wqa, Wqb, out):
                         nc.tensor.transpose(
                             out=xt[:, gg, u, :], in_=words[:, s % 2, col : col + P], identity=perm[:]
                         )
-                copy(
+                nc.scalar.copy(
                     out=xg_words[:, 2 * half : 2 * half + 2, :, :],
                     in_=xt[:].rearrange("p g u t -> p g t u"),
                 )
@@ -213,7 +209,7 @@ def tile_multilatentattention_pa_kernel(tc, x, Wqa, Wqb, out):
                         start=(g == 0),
                         stop=(g == G1 - 1),
                     )
-            cqg = work.tile([P, P, 4], BF16, name="cqg%d" % s, tag="cqg", bufs=2, align_bytes=64)
+            cqg = work.tile([P, P, 4], BF16, name="cqg%d" % s, tag="cqg", bufs=3, align_bytes=64)
             nc.scalar.copy(out=cqg[:], in_=cqp[:].rearrange("p c t -> p t c"))
             cq_grouped[s] = cqg
 
@@ -224,14 +220,23 @@ def tile_multilatentattention_pa_kernel(tc, x, Wqa, Wqb, out):
                 in_=cq_grouped[s][:].rearrange("p t c -> p (t c)"),
             )
 
-        def prepare_wb(g, kind, copy):
+        def both(step, j):
+            step(2 * j)
+            step(2 * j + 1)
+
+        wb_grouped = {}
+
+        def wb_regroup(g, kind, copy):
             wbg = work.tile([P, 512, 4], BF16, name="wbg", tag="wbg", bufs=2, align_bytes=64)
             src = wb_raw[g][:].rearrange("p t (h k c) -> p k h c t", h=HG, k=2)
             copy(out=wbg[:].rearrange("p (h c) t -> p h c t", h=HG), in_=src[:, kind])
+            wb_grouped[2 * g + kind] = wbg
+
+        def wb_quant(g, kind):
             nc.vector.quantize_mx(
                 out=wb_codes[2 * g + kind][:].bitcast(FP8X4),
                 scales=wb_scale[2 * g + kind][:],
-                in_=wbg[:].rearrange("p c t -> p (c t)"),
+                in_=wb_grouped[2 * g + kind][:].rearrange("p c t -> p (c t)"),
             )
 
         out_view = out.rearrange("b h (q s) f -> b q h s f", s=S)
@@ -249,104 +254,87 @@ def tile_multilatentattention_pa_kernel(tc, x, Wqa, Wqb, out):
             )
             return q_ps
 
-        results = {}
-
-        def nope_part(g, s):
-            if s % 4 == 0:
-                results[g] = work.tile([P, HG, 4, QH], F32, name="res", tag="res", bufs=4)
-            q_nope = second_matmul(g, 0, s)
-            nc.scalar.copy(
-                out=results[g][:, :, s % 4, 0:NOPE], in_=q_nope[:].rearrange("p (h c) -> p h c", h=HG)
-            )
-
-        def rope_part(g, s0):
+        def rotate(q_rope, s, part_a, part_b):
             shape = [P, HG, FREQ, 2]
-            part_a = work.tile([P, HG, 2, ROPE], F32, name="part_a", tag="part_a", bufs=3)
-            part_b = work.tile([P, HG, 2, ROPE], F32, name="part_b", tag="part_b", bufs=3)
-            for k in range(2):
-                s = s0 + k
-                q_rope = second_matmul(g, 1, s)
-                pairs = q_rope[:].rearrange("p (h m e) -> p h m e", h=HG, e=2)
-                nc.vector.tensor_tensor(
-                    out=part_a[:, :, k, :].rearrange("p h (m e) -> p h m e", e=2),
-                    in0=pairs[:, :, :, 0:1].to_broadcast(shape),
-                    in1=table[:, 1:3, s, :].rearrange("p e m -> p m e").unsqueeze(1).to_broadcast(shape),
-                    op=ALU.mult,
-                )
-                nc.vector.tensor_tensor(
-                    out=part_b[:, :, k, :].rearrange("p h (m e) -> p h m e", e=2),
-                    in0=pairs[:, :, :, 1:2].to_broadcast(shape),
-                    in1=table[:, 0:2, s, :].rearrange("p e m -> p m e").unsqueeze(1).to_broadcast(shape),
-                    op=ALU.mult,
-                )
-            nc.gpsimd.tensor_tensor(
-                out=results[g][:, :, s0 % 4 : s0 % 4 + 2, NOPE:QH], in0=part_a[:], in1=part_b[:], op=ALU.add
+            pairs = q_rope[:].rearrange("p (h m e) -> p h m e", h=HG, e=2)
+            nc.vector.tensor_tensor(
+                out=part_a[:, :, s % 2, :].rearrange("p h (m e) -> p h m e", e=2),
+                in0=pairs[:, :, :, 0:1].to_broadcast(shape),
+                in1=table[:, 1:3, s, :].rearrange("p e m -> p m e").unsqueeze(1).to_broadcast(shape),
+                op=ALU.mult,
+            )
+            nc.vector.tensor_tensor(
+                out=part_b[:, :, s % 2, :].rearrange("p h (m e) -> p h m e", e=2),
+                in0=pairs[:, :, :, 1:2].to_broadcast(shape),
+                in1=table[:, 0:2, s, :].rearrange("p e m -> p m e").unsqueeze(1).to_broadcast(shape),
+                op=ALU.mult,
             )
 
-        def store(g, s0, count):
+        def store(res, g, s0, count):
             for b in range(B):
                 nc.sync.dma_start(
                     out=out_view[b, :, HG * g : HG * (g + 1), s0 : s0 + count, :],
-                    in_=results[g][b::4, :, s0 % 4 : s0 % 4 + count, :],
+                    in_=res[b::4, :, s0 % 4 : s0 % 4 + count, :],
                 )
-
-        def tiles_in(s0, copy):
-            transpose_x(s0, copy)
-            transpose_x(s0 + 1, copy)
-            quant_x(s0)
-            quant_x(s0 + 1)
-
-        def tiles_through(s0):
-            first_matmul(s0)
-            first_matmul(s0 + 1)
-            quant_cq(s0)
-            quant_cq(s0 + 1)
-
-        def cells(g, s0):
-            nope_part(g, s0)
-            nope_part(g, s0 + 1)
-            rope_part(g, s0)
-            if s0 % 4 == 2:
-                store(g, s0 - 2, 4)
 
         by_scalar = nc.scalar.copy
         by_vector = nc.vector.tensor_copy
-        tiles_in(0, by_scalar)
-        prepare_wb(0, 1, by_scalar)
-        prepare_wb(0, 0, by_scalar)
-        prepare_wa()
-        tiles_through(0)
-        tiles_in(2, by_scalar)
-        cells(0, 0)
-        prepare_wb(1, 1, by_vector)
-        prepare_wb(1, 0, by_scalar)
-        cells(1, 0)
-        tiles_through(2)
-        tiles_in(4, by_scalar)
-        cells(0, 2)
-        cells(1, 2)
-        tiles_through(4)
-        tiles_in(6, by_scalar)
-        cells(0, 4)
-        prepare_wb(2, 1, by_scalar)
-        cells(1, 4)
-        tiles_through(6)
-        cells(0, 6)
-        prepare_wb(2, 0, by_scalar)
-        cells(1, 6)
-        for g in range(2, NG):
+
+        wa_regroup(0)
+        for g in range(1, G1):
+            wa_regroup(g)
+            wa_quant(g - 1)
+        wa_quant(G1 - 1)
+
+        both(transpose_x, 0)
+        both(quant_x, 0)
+        both(transpose_x, 1)
+        finish_tables()
+        both(first_matmul, 0)
+        both(quant_x, 1)
+        both(transpose_x, 2)
+        both(first_matmul, 1)
+        wb_regroup(0, 1, by_vector)
+        both(quant_cq, 0)
+        both(quant_x, 2)
+        both(transpose_x, 3)
+        both(first_matmul, 2)
+        wb_regroup(0, 0, by_vector)
+        wb_quant(0, 1)
+        both(quant_cq, 1)
+        wb_quant(0, 0)
+        both(quant_x, 3)
+        both(first_matmul, 3)
+        both(quant_cq, 2)
+        both(quant_cq, 3)
+
+        for g in range(NG):
             for sh in range(2):
-                for sl in range(4):
-                    nope_part(g, 4 * sh + sl)
-                if g + 1 < NG and sh == 0:
-                    prepare_wb(g + 1, 1, by_scalar)
-                    prepare_wb(g + 1, 0, by_scalar)
                 last = g == NG - 1 and sh == 1
-                rope_part(g, 4 * sh)
-                if last:
-                    store(g, 4 * sh, 2)
-                rope_part(g, 4 * sh + 2)
-                if last:
-                    store(g, 4 * sh + 2, 2)
-                else:
-                    store(g, 4 * sh, 4)
+                res = work.tile([P, HG, 4, QH], F32, name="res", tag="res", bufs=3)
+                ropes = []
+                for sl in range(4):
+                    s = 4 * sh + sl
+                    ropes.append(second_matmul(g, 1, s))
+                    q_nope = second_matmul(g, 0, s)
+                    nc.scalar.copy(
+                        out=res[:, :, sl, 0:NOPE], in_=q_nope[:].rearrange("p (h c) -> p h c", h=HG)
+                    )
+                if sh == 0 and g + 1 < NG:
+                    wb_regroup(g + 1, 1, by_scalar)
+                    wb_regroup(g + 1, 0, by_scalar)
+                for pair in range(2):
+                    part_a = work.tile([P, HG, 2, ROPE], F32, name="part_a", tag="part_a", bufs=3)
+                    part_b = work.tile([P, HG, 2, ROPE], F32, name="part_b", tag="part_b", bufs=3)
+                    for k in range(2):
+                        rotate(ropes[2 * pair + k], 4 * sh + 2 * pair + k, part_a, part_b)
+                    nc.gpsimd.tensor_tensor(
+                        out=res[:, :, 2 * pair : 2 * pair + 2, NOPE:QH], in0=part_a[:], in1=part_b[:], op=ALU.add
+                    )
+                    if last:
+                        store(res, g, 4 * sh + 2 * pair, 2)
+                    if pair == 0 and sh == 1 and g + 1 < NG:
+                        wb_quant(g + 1, 1)
+                        wb_quant(g + 1, 0)
+                if not last:
+                    store(res, g, 4 * sh, 4)

@@ -116,7 +116,7 @@ def tile_multilatentattention_pa_kernel(tc, x, Wqa, Wqb, out):
             nc.vector.tensor_scalar_mul(
                 out=theta[:, w : 2 * w], in0=theta[:, 0:w], scalar1=BASE ** (-2.0 * w / ROPE)
             )
-        scratch = work.tile([P, 6, S * FREQ], F32, name="scratch", tag="res", bufs=3)
+        scratch = work.tile([P, 6, S * FREQ], F32, name="scratch", tag="res", bufs=4)
         turns = scratch[:, 0, :]
         whole_i = scratch[:, 1, :].bitcast(I32)
         whole_f = scratch[:, 2, :]
@@ -310,8 +310,7 @@ def tile_multilatentattention_pa_kernel(tc, x, Wqa, Wqb, out):
 
         for g in range(NG):
             for sh in range(2):
-                last = g == NG - 1 and sh == 1
-                res = work.tile([P, HG, 4, QH], F32, name="res", tag="res", bufs=3)
+                res = work.tile([P, HG, 4, QH], F32, name="res", tag="res", bufs=4)
                 ropes = []
                 for sl in range(4):
                     s = 4 * sh + sl
@@ -331,10 +330,7 @@ def tile_multilatentattention_pa_kernel(tc, x, Wqa, Wqb, out):
                     nc.gpsimd.tensor_tensor(
                         out=res[:, :, 2 * pair : 2 * pair + 2, NOPE:QH], in0=part_a[:], in1=part_b[:], op=ALU.add
                     )
-                    if last:
-                        store(res, g, 4 * sh + 2 * pair, 2)
+                    store(res, g, 4 * sh + 2 * pair, 2)
                     if pair == 0 and sh == 1 and g + 1 < NG:
                         wb_quant(g + 1, 1)
                         wb_quant(g + 1, 0)
-                if not last:
-                    store(res, g, 4 * sh, 4)

@@ -123,7 +123,8 @@ def tile_multilatentattention_pa_kernel(tc, x, Wqa, Wqb, out):
         turns_c = scratch[:, 3, :]
         fold_s = scratch[:, 4, :]
         fold_c = scratch[:, 5, :]
-        table = keep.tile([P, 3, S, FREQ], F32, name="table")
+        planes = work.tile([P, 4, S * FREQ], F32, name="planes", tag="res", bufs=4)
+        table = keep.tile([P, S, FREQ, 4], F32, name="table")
         nc.vector.tensor_tensor(
             out=turns.rearrange("p (s m) -> p s m", s=S),
             in0=theta[:].unsqueeze(1).to_broadcast([P, S, FREQ]),
@@ -142,13 +143,13 @@ def tile_multilatentattention_pa_kernel(tc, x, Wqa, Wqb, out):
             nc.vector.scalar_tensor_tensor(
                 out=fold_c, in0=turns_c, scalar=0.5, in1=turns_c, op0=ALU.is_gt, op1=ALU.subtract
             )
-            for plane, src, sign in ((2, fold_s, -1.0), (0, fold_s, 1.0), (1, fold_c, -1.0)):
-                nc.scalar.activation(
-                    out=table[:, plane].rearrange("p s m -> p (s m)"),
-                    in_=src,
-                    func=ACT.Sin,
-                    scale=sign * 2.0 * math.pi,
-                )
+            for plane, src, sign in ((0, fold_c, -1.0), (1, fold_s, -1.0), (2, fold_s, 1.0), (3, fold_c, -1.0)):
+                nc.scalar.activation(out=planes[:, plane, :], in_=src, func=ACT.Sin, scale=sign * 2.0 * math.pi)
+
+        def interleave_tables():
+            nc.vector.tensor_copy(
+                out=table[:].rearrange("p s m q -> p (s m) q"), in_=planes[:].rearrange("p q x -> p x q")
+            )
 
         wa_grouped = []
 
@@ -254,19 +255,12 @@ def tile_multilatentattention_pa_kernel(tc, x, Wqa, Wqb, out):
             )
             return q_ps
 
-        def rotate(q_rope, s, part_a, part_b):
-            shape = [P, HG, FREQ, 2]
-            pairs = q_rope[:].rearrange("p (h m e) -> p h m e", h=HG, e=2)
+        def rotate(q_rope, s, products):
+            shape = [P, HG, ROPE, 2]
             nc.vector.tensor_tensor(
-                out=part_a[:, :, s % 2, :].rearrange("p h (m e) -> p h m e", e=2),
-                in0=pairs[:, :, :, 0:1].to_broadcast(shape),
-                in1=table[:, 1:3, s, :].rearrange("p e m -> p m e").unsqueeze(1).to_broadcast(shape),
-                op=ALU.mult,
-            )
-            nc.vector.tensor_tensor(
-                out=part_b[:, :, s % 2, :].rearrange("p h (m e) -> p h m e", e=2),
-                in0=pairs[:, :, :, 1:2].to_broadcast(shape),
-                in1=table[:, 0:2, s, :].rearrange("p e m -> p m e").unsqueeze(1).to_broadcast(shape),
+                out=products[:, :, s % 2, :].rearrange("p h (x e) -> p h x e", e=2),
+                in0=q_rope[:].rearrange("p (h x) -> p h x", h=HG).unsqueeze(3).to_broadcast(shape),
+                in1=table[:, s].rearrange("p m (j e) -> p (m j) e", e=2).unsqueeze(1).to_broadcast(shape),
                 op=ALU.mult,
             )
 
@@ -294,6 +288,7 @@ def tile_multilatentattention_pa_kernel(tc, x, Wqa, Wqb, out):
         both(quant_x, 1)
         both(transpose_x, 2)
         both(first_matmul, 1)
+        interleave_tables()
         wb_regroup(0, 1, by_vector)
         both(quant_cq, 0)
         both(quant_x, 2)
@@ -323,12 +318,15 @@ def tile_multilatentattention_pa_kernel(tc, x, Wqa, Wqb, out):
                     wb_regroup(g + 1, 1, by_scalar)
                     wb_regroup(g + 1, 0, by_scalar)
                 for pair in range(2):
-                    part_a = work.tile([P, HG, 2, ROPE], F32, name="part_a", tag="part_a", bufs=3)
-                    part_b = work.tile([P, HG, 2, ROPE], F32, name="part_b", tag="part_b", bufs=3)
+                    products = work.tile([P, HG, 2, 2 * ROPE], F32, name="products", tag="products", bufs=3)
                     for k in range(2):
-                        rotate(ropes[2 * pair + k], 4 * sh + 2 * pair + k, part_a, part_b)
+                        rotate(ropes[2 * pair + k], 4 * sh + 2 * pair + k, products)
+                    terms = products[:].rearrange("p h k (m j e) -> p (h k) m j e", j=2, e=2)
                     nc.gpsimd.tensor_tensor(
-                        out=res[:, :, 2 * pair : 2 * pair + 2, NOPE:QH], in0=part_a[:], in1=part_b[:], op=ALU.add
+                        out=res[:, :, 2 * pair : 2 * pair + 2, NOPE:QH],
+                        in0=terms[:, :, :, 0, :],
+                        in1=terms[:, :, :, 1, :],
+                        op=ALU.add,
                     )
                     store(res, g, 4 * sh + 2 * pair, 2)
                     if pair == 0 and sh == 1 and g + 1 < NG:

@@ -319,16 +319,21 @@ def tile_multilatentattention_pa_kernel(tc, x, Wqa, Wqb, out):
                     wb_regroup(g + 1, 0, by_scalar)
                 for pair in range(2):
                     products = work.tile([P, HG, 2, 2 * ROPE], F32, name="products", tag="products", bufs=3)
-                    for k in range(2):
-                        rotate(ropes[2 * pair + k], 4 * sh + 2 * pair + k, products)
-                    terms = products[:].rearrange("p h k (m j e) -> p (h k) m j e", j=2, e=2)
-                    nc.gpsimd.tensor_tensor(
-                        out=res[:, :, 2 * pair : 2 * pair + 2, NOPE:QH],
-                        in0=terms[:, :, :, 0, :],
-                        in1=terms[:, :, :, 1, :],
-                        op=ALU.add,
-                    )
-                    store(res, g, 4 * sh + 2 * pair, 2)
+                    count = 1 if (g == NG - 1 and sh == 1 and pair == 1) else 2
+                    for first in range(0, 2, count):
+                        for k in range(first, first + count):
+                            rotate(ropes[2 * pair + k], 4 * sh + 2 * pair + k, products)
+                        terms = products[:, :, first : first + count, :].rearrange(
+                            "p h k (m j e) -> p (h k) m j e", j=2, e=2
+                        )
+                        sl = 2 * pair + first
+                        nc.gpsimd.tensor_tensor(
+                            out=res[:, :, sl : sl + count, NOPE:QH],
+                            in0=terms[:, :, :, 0, :],
+                            in1=terms[:, :, :, 1, :],
+                            op=ALU.add,
+                        )
+                        store(res, g, 4 * sh + sl, count)
                     if pair == 0 and sh == 1 and g + 1 < NG:
                         wb_quant(g + 1, 1)
                         wb_quant(g + 1, 0)

@@ -47,7 +47,7 @@ def tile_multilatentattention_pa_kernel(tc, x, Wqa, Wqb, out):
         wa_raw = []
         x_raw = []
         wb_raw = []
-        x_view = x.flatten_outer_dims().rearrange("(p s) k -> p s k", s=S)
+        x_view = x.rearrange("b (p s) k -> b p s k", s=2)
 
         def load_wa(half):
             wa = work.tile([P, 2, 2, 1024], BF16, name="wa_raw%d" % half, tag="raw8", bufs=6)
@@ -65,7 +65,7 @@ def tile_multilatentattention_pa_kernel(tc, x, Wqa, Wqb, out):
             for i in range(pieces):
                 nc.sync.dma_start(
                     out=xs[:, step * i : step * (i + 1), :],
-                    in_=x_view[:, 2 * sq + step * i : 2 * sq + step * (i + 1), :],
+                    in_=x_view[sq, :, step * i : step * (i + 1), :],
                 )
             x_raw.append(xs)
 
@@ -93,21 +93,10 @@ def tile_multilatentattention_pa_kernel(tc, x, Wqa, Wqb, out):
 
         ident = keep.tile([P, P], F32, name="ident")
         masks.make_identity(nc, ident[:])
-        two_p = keep.tile([P, S], I32, name="two_p")
-        nc.gpsimd.iota(two_p[:], pattern=[[0, S]], base=0, channel_multiplier=2)
-        s_idx = keep.tile([P, S], I32, name="s_idx")
-        nc.gpsimd.iota(s_idx[:], pattern=[[1, S]], base=0, channel_multiplier=0)
-
-        perm = keep.tile([P, P], F32, name="perm")
-        nc.vector.tensor_copy(
-            out=perm[:].rearrange("p (q b) -> p q b", b=B), in_=ident[:].rearrange("p (b q) -> p q b", b=B)
-        )
-        nc.vector.tensor_single_scalar(out=two_p[:], in_=two_p[:], scalar=248, op=ALU.bitwise_and)
-        pos_a = keep.tile([P, S], F32, name="pos_a")
-        nc.vector.tensor_copy(out=pos_a[:], in_=two_p[:])
-        pos_b = keep.tile([P, S], F32, name="pos_b")
-        nc.vector.tensor_copy(out=pos_b[:], in_=s_idx[:])
-        nc.vector.tensor_tensor(out=pos_a[:], in0=pos_a[:], in1=pos_b[:], op=ALU.add)
+        pos_i = keep.tile([P, 2], I32, name="pos_i")
+        nc.gpsimd.iota(pos_i[:], pattern=[[1, 2]], base=0, channel_multiplier=2)
+        pos_a = keep.tile([P, 2], F32, name="pos_a")
+        nc.vector.tensor_copy(out=pos_a[:], in_=pos_i[:])
         nc.vector.tensor_scalar_mul(out=pos_a[:], in0=pos_a[:], scalar1=1.0 / (2.0 * math.pi))
         theta = keep.tile([P, FREQ], F32, name="theta")
         nc.vector.memset(theta[:, 0:1], 1.0)
@@ -116,35 +105,34 @@ def tile_multilatentattention_pa_kernel(tc, x, Wqa, Wqb, out):
             nc.vector.tensor_scalar_mul(
                 out=theta[:, w : 2 * w], in0=theta[:, 0:w], scalar1=BASE ** (-2.0 * w / ROPE)
             )
-        scratch = work.tile([P, 6, S * FREQ], F32, name="scratch", tag="res", bufs=4)
+        scratch = keep.tile([P, 6, 2 * FREQ], F32, name="scratch")
         turns = scratch[:, 0, :]
         whole_i = scratch[:, 1, :].bitcast(I32)
         whole_f = scratch[:, 2, :]
         turns_c = scratch[:, 3, :]
         fold_s = scratch[:, 4, :]
         fold_c = scratch[:, 5, :]
-        planes = work.tile([P, 4, S * FREQ], F32, name="planes", tag="res", bufs=4)
-        table = keep.tile([P, S, FREQ, 4], F32, name="table")
+        planes = keep.tile([P, 4, 2 * FREQ], F32, name="planes")
+        table = keep.tile([P, 2, FREQ, 4], F32, name="table")
         nc.vector.tensor_tensor(
-            out=turns.rearrange("p (s m) -> p s m", s=S),
-            in0=theta[:].unsqueeze(1).to_broadcast([P, S, FREQ]),
-            in1=pos_a[:].unsqueeze(2).to_broadcast([P, S, FREQ]),
+            out=turns.rearrange("p (s m) -> p s m", s=2),
+            in0=theta[:].unsqueeze(1).to_broadcast([P, 2, FREQ]),
+            in1=pos_a[:].unsqueeze(2).to_broadcast([P, 2, FREQ]),
             op=ALU.mult,
         )
         nc.vector.tensor_copy(out=whole_i, in_=turns)
         nc.vector.tensor_copy(out=whole_f, in_=whole_i)
 
-        def finish_tables():
-            nc.vector.tensor_tensor(out=turns, in0=turns, in1=whole_f, op=ALU.subtract)
-            nc.vector.tensor_scalar_add(out=turns_c, in0=turns, scalar1=0.25)
-            nc.vector.scalar_tensor_tensor(
-                out=fold_s, in0=turns, scalar=0.5, in1=turns, op0=ALU.is_gt, op1=ALU.subtract
-            )
-            nc.vector.scalar_tensor_tensor(
-                out=fold_c, in0=turns_c, scalar=0.5, in1=turns_c, op0=ALU.is_gt, op1=ALU.subtract
-            )
-            for plane, src, sign in ((0, fold_c, -1.0), (1, fold_s, -1.0), (2, fold_s, 1.0), (3, fold_c, -1.0)):
-                nc.scalar.activation(out=planes[:, plane, :], in_=src, func=ACT.Sin, scale=sign * 2.0 * math.pi)
+        nc.vector.tensor_tensor(out=turns, in0=turns, in1=whole_f, op=ALU.subtract)
+        nc.vector.tensor_scalar_add(out=turns_c, in0=turns, scalar1=0.25)
+        nc.vector.scalar_tensor_tensor(
+            out=fold_s, in0=turns, scalar=0.5, in1=turns, op0=ALU.is_gt, op1=ALU.subtract
+        )
+        nc.vector.scalar_tensor_tensor(
+            out=fold_c, in0=turns_c, scalar=0.5, in1=turns_c, op0=ALU.is_gt, op1=ALU.subtract
+        )
+        for plane, src, sign in ((0, fold_c, -1.0), (1, fold_s, -1.0), (2, fold_s, 1.0), (3, fold_c, -1.0)):
+            nc.scalar.activation(out=planes[:, plane, :], in_=src, func=ACT.Sin, scale=sign * 2.0 * math.pi)
 
         def interleave_tables():
             nc.vector.tensor_copy(
@@ -182,7 +170,7 @@ def tile_multilatentattention_pa_kernel(tc, x, Wqa, Wqb, out):
                     for u in range(2):
                         col = 256 * (2 * half + gg) + 128 * u
                         nc.tensor.transpose(
-                            out=xt[:, gg, u, :], in_=words[:, s % 2, col : col + P], identity=perm[:]
+                            out=xt[:, gg, u, :], in_=words[:, s % 2, col : col + P], identity=ident[:]
                         )
                 nc.scalar.copy(
                     out=xg_words[:, 2 * half : 2 * half + 2, :, :],
@@ -240,7 +228,7 @@ def tile_multilatentattention_pa_kernel(tc, x, Wqa, Wqb, out):
                 in_=wb_grouped[2 * g + kind][:].rearrange("p c t -> p (c t)"),
             )
 
-        out_view = out.rearrange("b h (q s) f -> b q h s f", s=S)
+        out_view = out.rearrange("b h (p s) f -> b p h s f", s=2)
 
         def second_matmul(g, kind, s):
             q_ps = psum.tile([P, 512], F32, name="q_ps", tag="ps")
@@ -260,16 +248,14 @@ def tile_multilatentattention_pa_kernel(tc, x, Wqa, Wqb, out):
             nc.vector.tensor_tensor(
                 out=products[:, :, s % 2, :].rearrange("p h (x e) -> p h x e", e=2),
                 in0=q_rope[:].rearrange("p (h x) -> p h x", h=HG).unsqueeze(3).to_broadcast(shape),
-                in1=table[:, s].rearrange("p m (j e) -> p (m j) e", e=2).unsqueeze(1).to_broadcast(shape),
+                in1=table[:, s % 2].rearrange("p m (j e) -> p (m j) e", e=2).unsqueeze(1).to_broadcast(shape),
                 op=ALU.mult,
             )
 
-        def store(res, g, s0, count):
-            for b in range(B):
-                nc.sync.dma_start(
-                    out=out_view[b, :, HG * g : HG * (g + 1), s0 : s0 + count, :],
-                    in_=res[b::4, :, s0 % 4 : s0 % 4 + count, :],
-                )
+        def store(res, g, s0):
+            nc.sync.dma_start(
+                out=out_view[s0 // 2, :, HG * g : HG * (g + 1), :, :], in_=res[:, :, s0 % 4 : s0 % 4 + 2, :]
+            )
 
         by_scalar = nc.scalar.copy
         by_vector = nc.vector.tensor_copy
@@ -280,15 +266,14 @@ def tile_multilatentattention_pa_kernel(tc, x, Wqa, Wqb, out):
             wa_quant(g - 1)
         wa_quant(G1 - 1)
 
+        interleave_tables()
         both(transpose_x, 0)
         both(quant_x, 0)
         both(transpose_x, 1)
-        finish_tables()
         both(first_matmul, 0)
         both(quant_x, 1)
         both(transpose_x, 2)
         both(first_matmul, 1)
-        interleave_tables()
         wb_regroup(0, 1, by_vector)
         both(quant_cq, 0)
         both(quant_x, 2)
@@ -319,21 +304,16 @@ def tile_multilatentattention_pa_kernel(tc, x, Wqa, Wqb, out):
                     wb_regroup(g + 1, 0, by_scalar)
                 for pair in range(2):
                     products = work.tile([P, HG, 2, 2 * ROPE], F32, name="products", tag="products", bufs=3)
-                    count = 1 if (g == NG - 1 and sh == 1 and pair == 1) else 2
-                    for first in range(0, 2, count):
-                        for k in range(first, first + count):
-                            rotate(ropes[2 * pair + k], 4 * sh + 2 * pair + k, products)
-                        terms = products[:, :, first : first + count, :].rearrange(
-                            "p h k (m j e) -> p (h k) m j e", j=2, e=2
-                        )
-                        sl = 2 * pair + first
-                        nc.gpsimd.tensor_tensor(
-                            out=res[:, :, sl : sl + count, NOPE:QH],
-                            in0=terms[:, :, :, 0, :],
-                            in1=terms[:, :, :, 1, :],
-                            op=ALU.add,
-                        )
-                        store(res, g, 4 * sh + sl, count)
+                    for k in range(2):
+                        rotate(ropes[2 * pair + k], 4 * sh + 2 * pair + k, products)
+                    terms = products[:].rearrange("p h k (m j e) -> p (h k) m j e", j=2, e=2)
+                    nc.gpsimd.tensor_tensor(
+                        out=res[:, :, 2 * pair : 2 * pair + 2, NOPE:QH],
+                        in0=terms[:, :, :, 0, :],
+                        in1=terms[:, :, :, 1, :],
+                        op=ALU.add,
+                    )
+                    store(res, g, 4 * sh + 2 * pair)
                     if pair == 0 and sh == 1 and g + 1 < NG:
                         wb_quant(g + 1, 1)
                         wb_quant(g + 1, 0)

@@ -33,7 +33,6 @@ def tile_multilatentattention_pa_kernel(tc, x, Wqa, Wqb, out):
         keep = ctx.enter_context(tc.tile_pool(name="keep", bufs=1))
         work = ctx.enter_context(tc.tile_pool(name="work", bufs=2))
         psum = ctx.enter_context(tc.psum_pool(name="psum", bufs=8))
-        ctx.enter_context(tc.manual_schedule())
 
         wa_codes = [keep.tile([P, QR], U32, name="wa_codes%d" % g, align_bytes=64) for g in range(G1)]
         wa_scale = [keep.tile([P, QR], U8, name="wa_scale%d" % g, align_bytes=64) for g in range(G1)]

import math
from contextlib import ExitStack

import concourse.masks as masks
import concourse.mybir as mybir

F32 = mybir.dt.float32
BF16 = mybir.dt.bfloat16
U32 = mybir.dt.uint32
U8 = mybir.dt.uint8
I32 = mybir.dt.int32
FP8X4 = mybir.dt.float8_e4m3fn_x4
ALU = mybir.AluOpType
ACT = mybir.ActivationFunctionType

P = 128
B, N, E, H, QR = 4, 256, 2048, 16, 512
NOPE, ROPE = 128, 128
QH = NOPE + ROPE
BASE = 10000.0
S = 8
G1 = E // 512
HG = 4
NG = H // HG
FREQ = ROPE // 2

FLOPS = 2 * B * N * E * QR + 2 * B * N * QR * H * QH


def tile_multilatentattention_pa_kernel(tc, x, Wqa, Wqb, out):
    nc = tc.nc
    with ExitStack() as ctx:
        keep = ctx.enter_context(tc.tile_pool(name="keep", bufs=1))
        work = ctx.enter_context(tc.tile_pool(name="work", bufs=2))
        psum = ctx.enter_context(tc.psum_pool(name="psum", bufs=8))

        wa_codes = [keep.tile([P, QR], U32, name="wa_codes%d" % g, align_bytes=64) for g in range(G1)]
        wa_scale = [keep.tile([P, QR], U8, name="wa_scale%d" % g, align_bytes=64) for g in range(G1)]
        x_codes = [keep.tile([P, G1 * P], U32, name="x_codes%d" % s, align_bytes=64) for s in range(S)]
        x_scale = [keep.tile([P, G1 * P], U8, name="x_scale%d" % s, align_bytes=64) for s in range(S)]
        cq_codes = [keep.tile([P, P], U32, name="cq_codes%d" % s, align_bytes=64) for s in range(S)]
        cq_scale = [keep.tile([P, P], U8, name="cq_scale%d" % s, align_bytes=64) for s in range(S)]
        wb_codes = [keep.tile([P, 512], U32, name="wb_codes%d" % i, align_bytes=64) for i in range(2 * NG)]
        wb_scale = [keep.tile([P, 512], U8, name="wb_scale%d" % i, align_bytes=64) for i in range(2 * NG)]

        wa_raw = []
        x_raw = []
        wb_raw = []
        x_view = x.rearrange("b (p s) k -> b p s k", s=2)

        def load_wa(half):
            wa = work.tile([P, 2, 2, 1024], BF16, name="wa_raw%d" % half, tag="raw8", bufs=6)
            for gg in range(2):
                g = 2 * half + gg
                nc.sync.dma_start(
                    out=wa[:, gg],
                    in_=Wqa[512 * g : 512 * (g + 1), :].rearrange("(u p e) c -> p u (e c)", u=2, e=2),
                )
            wa_raw.append(wa)

        def load_x(sq, pieces):
            xs = work.tile([P, 2, E], BF16, name="x_raw%d" % sq, tag="raw8", bufs=6)
            step = 2 // pieces
            for i in range(pieces):
                nc.sync.dma_start(
                    out=xs[:, step * i : step * (i + 1), :],
                    in_=x_view[sq, :, step * i : step * (i + 1), :],
                )
            x_raw.append(xs)

        def load_wb(g):
            wb = work.tile([P, 4, 1024], BF16, name="wb_raw%d" % g, tag="raw8", bufs=6)
            nc.sync.dma_start(
                out=wb[:], in_=Wqb[:, 1024 * g : 1024 * (g + 1)].rearrange("(t p) c -> p t c", t=4)
            )
            wb_raw.append(wb)

        load_wa(0)
        load_wa(1)
        load_x(0, 2)
        load_x(1, 1)
        load_x(2, 1)
        load_wb(0)
        load_x(3, 1)
        load_wb(1)
        load_wb(2)
        load_wb(3)

        warm = keep.tile([P, 1], F32, name="warm")
        nc.vector.memset(warm[:], 0.0)
        nc.scalar.activation(out=warm[:], in_=warm[:], func=ACT.Sin)

        ident = keep.tile([P, P], F32, name="ident")
        masks.make_identity(nc, ident[:])
        pos_i = keep.tile([P, 2], I32, name="pos_i")
        nc.gpsimd.iota(pos_i[:], pattern=[[1, 2]], base=0, channel_multiplier=2)
        pos_a = keep.tile([P, 2], F32, name="pos_a")
        nc.vector.tensor_copy(out=pos_a[:], in_=pos_i[:])
        nc.vector.tensor_scalar_mul(out=pos_a[:], in0=pos_a[:], scalar1=1.0 / (2.0 * math.pi))
        theta = keep.tile([P, FREQ], F32, name="theta")
        nc.vector.memset(theta[:, 0:1], 1.0)
        for j in range(6):
            w = 1 << j
            nc.vector.tensor_scalar_mul(
                out=theta[:, w : 2 * w], in0=theta[:, 0:w], scalar1=BASE ** (-2.0 * w / ROPE)
            )
        scratch = keep.tile([P, 6, 2 * FREQ], F32, name="scratch")
        turns = scratch[:, 0, :]
        whole_i = scratch[:, 1, :].bitcast(I32)
        whole_f = scratch[:, 2, :]
        turns_c = scratch[:, 3, :]
        fold_s = scratch[:, 4, :]
        fold_c = scratch[:, 5, :]
        planes = keep.tile([P, 4, 2 * FREQ], F32, name="planes")
        table = keep.tile([P, 2, FREQ, 4], F32, name="table")
        nc.vector.tensor_tensor(
            out=turns.rearrange("p (s m) -> p s m", s=2),
            in0=theta[:].unsqueeze(1).to_broadcast([P, 2, FREQ]),
            in1=pos_a[:].unsqueeze(2).to_broadcast([P, 2, FREQ]),
            op=ALU.mult,
        )
        nc.vector.tensor_copy(out=whole_i, in_=turns)
        nc.vector.tensor_copy(out=whole_f, in_=whole_i)

        nc.vector.tensor_tensor(out=turns, in0=turns, in1=whole_f, op=ALU.subtract)
        nc.vector.tensor_scalar_add(out=turns_c, in0=turns, scalar1=0.25)
        nc.vector.scalar_tensor_tensor(
            out=fold_s, in0=turns, scalar=0.5, in1=turns, op0=ALU.is_gt, op1=ALU.subtract
        )
        nc.vector.scalar_tensor_tensor(
            out=fold_c, in0=turns_c, scalar=0.5, in1=turns_c, op0=ALU.is_gt, op1=ALU.subtract
        )
        for plane, src, sign in ((0, fold_c, -1.0), (1, fold_s, -1.0), (2, fold_s, 1.0), (3, fold_c, -1.0)):
            nc.scalar.activation(out=planes[:, plane, :], in_=src, func=ACT.Sin, scale=sign * 2.0 * math.pi)

        def interleave_tables():
            nc.vector.tensor_copy(
                out=table[:].rearrange("p s m q -> p (s m) q"), in_=planes[:].rearrange("p q x -> p x q")
            )

        wa_grouped = []

        def wa_regroup(g):
            wag = work.tile([P, QR, 4], BF16, name="wag%d" % g, tag="wag", bufs=2, align_bytes=64)
            src = wa_raw[g // 2][:, g % 2].rearrange("p u (e c) -> p (u e) c", e=2)
            nc.vector.tensor_copy(
                out=wag[:].rearrange("p (c i) t -> p c t i", i=4),
                in_=src.rearrange("p t (c i) -> p c t i", i=4),
            )
            wa_grouped.append(wag)

        def wa_quant(g):
            nc.vector.quantize_mx(
                out=wa_codes[g][:].bitcast(FP8X4),
                scales=wa_scale[g][:],
                in_=wa_grouped[g][:].rearrange("p c t -> p (c t)"),
            )

        x_grouped = {}
        cq_grouped = {}

        def transpose_x(s):
            words = x_raw[s // 2][:].bitcast(F32)
            xg = work.tile([P, G1, P, 4], BF16, name="xg%d" % s, tag="xg", bufs=3, align_bytes=64)
            xg_words = xg[:].bitcast(F32)
            for half in range(2):
                xt = psum.tile([P, 2, 2, P], F32, name="xt", tag="ps")
                for gg in range(2):
                    for u in range(2):
                        col = 256 * (2 * half + gg) + 128 * u
                        nc.tensor.transpose(
                            out=xt[:, gg, u, :], in_=words[:, s % 2, col : col + P], identity=ident[:]
                        )
                nc.scalar.copy(
                    out=xg_words[:, 2 * half : 2 * half + 2, :, :],
                    in_=xt[:].rearrange("p g u t -> p g t u"),
                )
            x_grouped[s] = xg

        def quant_x(s):
            nc.vector.quantize_mx(
                out=x_codes[s][:].bitcast(FP8X4),
                scales=x_scale[s][:],
                in_=x_grouped[s][:].rearrange("p g t j -> p (g t j)"),
            )

        def first_matmul(s):
            cqp = psum.tile([P, 4, P], F32, name="cqp", tag="ps")
            for c in range(4):
                for g in range(G1):
                    nc.tensor.matmul_mx(
                        out=cqp[:, c, :],
                        lhsT=wa_codes[g][:, P * c : P * (c + 1)].bitcast(FP8X4),
                        lhsT_scale=wa_scale[g][:, P * c : P * (c + 1)],
                        rhs=x_codes[s][:, P * g : P * (g + 1)].bitcast(FP8X4),
                        rhs_scale=x_scale[s][:, P * g : P * (g + 1)],
                        start=(g == 0),
                        stop=(g == G1 - 1),
                    )
            cqg = work.tile([P, P, 4], BF16, name="cqg%d" % s, tag="cqg", bufs=3, align_bytes=64)
            nc.scalar.copy(out=cqg[:], in_=cqp[:].rearrange("p c t -> p t c"))
            cq_grouped[s] = cqg

        def quant_cq(s):
            nc.vector.quantize_mx(
                out=cq_codes[s][:].bitcast(FP8X4),
                scales=cq_scale[s][:],
                in_=cq_grouped[s][:].rearrange("p t c -> p (t c)"),
            )

        def both(step, j):
            step(2 * j)
            step(2 * j + 1)

        wb_grouped = {}

        def wb_regroup(g, kind, copy):
            wbg = work.tile([P, 512, 4], BF16, name="wbg", tag="wbg", bufs=2, align_bytes=64)
            src = wb_raw[g][:].rearrange("p t (h k c) -> p k h c t", h=HG, k=2)
            copy(out=wbg[:].rearrange("p (h c) t -> p h c t", h=HG), in_=src[:, kind])
            wb_grouped[2 * g + kind] = wbg

        def wb_quant(g, kind):
            nc.vector.quantize_mx(
                out=wb_codes[2 * g + kind][:].bitcast(FP8X4),
                scales=wb_scale[2 * g + kind][:],
                in_=wb_grouped[2 * g + kind][:].rearrange("p c t -> p (c t)"),
            )

        out_view = out.rearrange("b h (p s) f -> b p h s f", s=2)

        def second_matmul(g, kind, s):
            q_ps = psum.tile([P, 512], F32, name="q_ps", tag="ps")
            nc.tensor.matmul_mx(
                out=q_ps[:],
                lhsT=cq_codes[s][:].bitcast(FP8X4),
                lhsT_scale=cq_scale[s][:],
                rhs=wb_codes[2 * g + kind][:].bitcast(FP8X4),
                rhs_scale=wb_scale[2 * g + kind][:],
                start=True,
                stop=True,
            )
            return q_ps

        def rotate(q_rope, s, products):
            shape = [P, HG, ROPE, 2]
            nc.vector.tensor_tensor(
                out=products[:, :, s % 2, :].rearrange("p h (x e) -> p h x e", e=2),
                in0=q_rope[:].rearrange("p (h x) -> p h x", h=HG).unsqueeze(3).to_broadcast(shape),
                in1=table[:, s % 2].rearrange("p m (j e) -> p (m j) e", e=2).unsqueeze(1).to_broadcast(shape),
                op=ALU.mult,
            )

        def store(res, g, s0):
            nc.sync.dma_start(
                out=out_view[s0 // 2, :, HG * g : HG * (g + 1), :, :], in_=res[:, :, s0 % 4 : s0 % 4 + 2, :]
            )

        by_scalar = nc.scalar.copy
        by_vector = nc.vector.tensor_copy

        wa_regroup(0)
        for g in range(1, G1):
            wa_regroup(g)
            wa_quant(g - 1)
        wa_quant(G1 - 1)

        interleave_tables()
        both(transpose_x, 0)
        both(quant_x, 0)
        both(transpose_x, 1)
        both(first_matmul, 0)
        both(quant_x, 1)
        both(transpose_x, 2)
        both(first_matmul, 1)
        wb_regroup(0, 1, by_vector)
        both(quant_cq, 0)
        both(quant_x, 2)
        both(transpose_x, 3)
        both(first_matmul, 2)
        wb_regroup(0, 0, by_vector)
        wb_quant(0, 1)
        both(quant_cq, 1)
        wb_quant(0, 0)
        both(quant_x, 3)
        both(first_matmul, 3)
        both(quant_cq, 2)
        both(quant_cq, 3)

        for g in range(NG):
            for sh in range(2):
                res = work.tile([P, HG, 4, QH], F32, name="res", tag="res", bufs=4)
                ropes = []
                for sl in range(4):
                    s = 4 * sh + sl
                    ropes.append(second_matmul(g, 1, s))
                    q_nope = second_matmul(g, 0, s)
                    nc.scalar.copy(
                        out=res[:, :, sl, 0:NOPE], in_=q_nope[:].rearrange("p (h c) -> p h c", h=HG)
                    )
                if sh == 0 and g + 1 < NG:
                    wb_regroup(g + 1, 1, by_scalar)
                    wb_regroup(g + 1, 0, by_scalar)
                for pair in range(2):
                    products = work.tile([P, HG, 2, 2 * ROPE], F32, name="products", tag="products", bufs=3)
                    for k in range(2):
                        rotate(ropes[2 * pair + k], 4 * sh + 2 * pair + k, products)
                    terms = products[:].rearrange("p h k (m j e) -> p (h k) m j e", j=2, e=2)
                    nc.gpsimd.tensor_tensor(
                        out=res[:, :, 2 * pair : 2 * pair + 2, NOPE:QH],
                        in0=terms[:, :, :, 0, :],
                        in1=terms[:, :, :, 1, :],
                        op=ALU.add,
                    )
                    store(res, g, 4 * sh + 2 * pair)
                    if pair == 0 and sh == 1 and g + 1 < NG:
                        wb_quant(g + 1, 1)
                        wb_quant(g + 1, 0)
